import numpy as np
import ml_dtypes


def mxq(x, axis, fmt="e4m3"):
    dtype, down = {"e4m3": (ml_dtypes.float8_e4m3fn, 7), "e5m2": (ml_dtypes.float8_e5m2, 14)}[fmt]
    v = np.moveaxis(np.asarray(x, np.float32).astype(ml_dtypes.bfloat16).astype(np.float64), axis, -1)
    blocks = v.reshape(v.shape[:-1] + (-1, 32))
    amax = np.abs(blocks).max(-1, keepdims=True)
    byte = np.maximum(np.where(amax > 0, np.frexp(amax)[1] - 1 + 127, 0) - down, 1)
    scale = np.exp2(byte - 127.0)
    codes = (blocks / scale).astype(np.float32).astype(dtype).astype(np.float64)
    return np.moveaxis((codes * scale).reshape(v.shape), -1, axis)


WIDE = False


def mx_kscale(k):
    if not WIDE:
        return np.ones(k)
    levels = np.array([30, -30])
    if k % 512:
        return np.exp2(np.random.permutation(np.resize(levels, k // 32))).repeat(32)
    a = np.empty((k // 512, 16))
    for p in range(k // 512):
        a[p, :8] = np.random.permutation(np.resize(levels, 8))
        for g in range(8):
            far = levels[np.abs(levels - a[p, g]) >= 10]
            a[p, g + 8] = far[np.random.randint(len(far))]
    return np.exp2(a.ravel()).repeat(32)


BF16 = ml_dtypes.bfloat16


def bf(x):
    return np.asarray(x, np.float32).astype(BF16)


def f64(x):
    return np.asarray(x).astype(np.float64)


E2M1 = np.array([0.0, 0.5, 1.0, 1.5, 2.0, 3.0, 4.0, 6.0, -0.0, -0.5, -1.0, -1.5, -2.0, -3.0, -4.0, -6.0])


def pack_weight(w, fmt):
    k, n = w.shape
    w = f64(bf(w)).reshape(k // 32, 32, n)
    amax = np.abs(w).max(1)
    if fmt == "e4m3":
        byte = np.frexp(amax)[1] - 1 + 127 - 7
    else:
        mant, ex = np.frexp(amax / 6.0)
        byte = np.where(mant > 0.5, ex, ex - 1) + 127
    byte = np.clip(np.where(amax > 0, byte, 1), 1, 254)
    scaled = (w * np.exp2(127.0 - byte)[:, None, :]).reshape(k, n).astype(np.float32)
    by_word = np.ascontiguousarray(scaled.reshape(k // 512, 128, 4, n).transpose(0, 1, 3, 2))
    if fmt == "e4m3":
        words = by_word.astype(ml_dtypes.float8_e4m3fn).view(np.uint8)
    else:
        c = by_word.astype(ml_dtypes.float4_e2m1fn).view(np.uint8) & 0xF
        words = c[..., 0::2] | (c[..., 1::2] << 4)
    return np.ascontiguousarray(words), np.ascontiguousarray(byte.astype(np.uint8).reshape(k // 512, 16, n))


def unpack_weight(words, scales, fmt):
    g, p, n, _ = words.shape
    if fmt == "e4m3":
        vals = np.ascontiguousarray(words).view(ml_dtypes.float8_e4m3fn).astype(np.float64)
    else:
        nib = np.empty((g, p, n, 4), np.uint8)
        nib[..., 0::2] = words & 0xF
        nib[..., 1::2] = words >> 4
        vals = E2M1[nib]
    vals = vals * np.repeat(np.exp2(scales.astype(np.float64) - 127.0), 8, axis=1)[..., None]
    return vals.transpose(0, 1, 3, 2).reshape(g * 512, n)

def pack4(w):
    words, scales = pack_weight(w, "e2m1")
    return words.reshape(words.shape[0], 128, -1), scales


def unpack4(words, scales):
    return unpack_weight(words.reshape(words.shape[0], 128, -1, 2), scales, "e2m1")


B, HH, WW, C, NH, DIM = 2, 16, 32, 512, 8, 128
N = HH * WW
HD = NH * DIM
F = 4 * HD
BN_EPS = 1e-5
WS = 0.02
GQK = np.sqrt(2.8) / DIM ** 0.25
GV = 4.0


def heads(t):
    return t.reshape(B, N, NH, DIM).transpose(0, 2, 1, 3)


def setup_inputs():
    s = mx_kscale(C)
    x = np.random.standard_normal((B, HH, WW, C)) + 0.5 * np.random.standard_normal(C)
    gain = np.concatenate([np.full(2 * HD, GQK), np.full(2 * HD, GV)])
    inputs = bf(x * s)
    words, scales = pack4(np.random.standard_normal((C, F)) * WS / np.sqrt(C) / s[:, None])
    return {"inputs": inputs,
            "w_qkv_words": words,
            "w_qkv_scales": scales,
            "bn_scale": bf(np.random.standard_normal(F) * gain)}


def reference(inputs, w_qkv_words, w_qkv_scales, bn_scale):
    x = mxq(f64(inputs).reshape(B * N, C), 1, "e5m2") @ unpack4(w_qkv_words, w_qkv_scales)
    mean = x.mean(axis=0)
    var = x.var(axis=0)
    x = (x - mean) / np.sqrt(var + BN_EPS) * f64(bn_scale)
    q, k, v1, v2 = (heads(t) for t in np.split(x.reshape(B, N, F), 4, axis=-1))
    v = np.concatenate((v1, v2), axis=-1)
    return np.ascontiguousarray(q), np.ascontiguousarray(k), v

@@ -1,0 +1,217 @@
+from contextlib import ExitStack
+
+import concourse.mybir as mybir
+from concourse.masks import make_identity
+
+MAPS, PIXELS, K, HEADS, DIM = 2, 512, 512, 8, 128
+COLUMNS = 4 * HEADS * DIM
+BN_EPS = 1e-5
+FLOPS = 2 * MAPS * PIXELS * K * COLUMNS
+
+F32 = mybir.dt.float32
+BF16 = mybir.dt.bfloat16
+I32 = mybir.dt.int32
+U32 = mybir.dt.uint32
+U8 = mybir.dt.uint8
+E5M2X4 = mybir.dt.float8_e5m2_x4
+E2M1X4 = mybir.dt.float4_e2m1fn_x4
+ALU = mybir.AluOpType
+ACT = mybir.ActivationFunctionType
+
+P = 128
+ROWS = PIXELS // P
+QUARTER = HEADS * DIM
+TILES = COLUMNS // P
+Q_PART, K_PART, V1_PART, V2_PART = range(4)
+
+
+def tile_levitattention_pa_kernel(tc, inputs, w_qkv_words, w_qkv_scales, bn_scale, out_0, out_1, out_2):
+    nc = tc.nc
+
+    order = [(Q_PART, h) for h in range(HEADS)]
+    for h in range(HEADS):
+        order += [(V1_PART, h), (V2_PART, h)]
+    order += [(K_PART, h) for h in range(HEADS)]
+
+    with ExitStack() as ctx:
+        keep = ctx.enter_context(tc.tile_pool(name="keep", bufs=1))
+        small = ctx.enter_context(tc.tile_pool(name="small", bufs=4))
+        work = ctx.enter_context(tc.tile_pool(name="work", bufs=4))
+        product_banks = ctx.enter_context(tc.psum_pool(name="product_banks", bufs=6))
+        turned_banks = ctx.enter_context(tc.psum_pool(name="turned_banks", bufs=2))
+        ctx.enter_context(tc.manual_schedule())
+
+        pixels = inputs.rearrange("b h w c -> b (h w) c")
+        x_rows = []
+        for i in range(2 * MAPS):
+            b, half = divmod(i, 2)
+            rows = keep.tile([P, 2, K], BF16, name="x_rows%d" % i, align_bytes=64)
+            nc.sync.dma_start(out=rows[:], in_=pixels[b].rearrange("(p j) c -> p j c", j=ROWS)[:, 2 * half : 2 * half + 2, :])
+            x_rows.append(rows)
+
+        gain_rows = keep.tile([TILES, P], BF16, name="gain_rows")
+        nc.scalar.dma_start(out=gain_rows[:], in_=bn_scale.rearrange("(c p) -> c p", p=P))
+
+        first_scales = keep.tile([P, QUARTER], U8, name="first_scales", align_bytes=64)
+        other_scales = keep.tile([P, COLUMNS - QUARTER], U8, name="other_scales", align_bytes=64)
+        nc.vector.memset(first_scales[:].bitcast(I32), 0)
+        nc.vector.memset(other_scales[:].bitcast(I32), 0)
+
+        ident = keep.tile([P, P], F32, name="ident")
+        make_identity(nc, ident[:])
+        gain_square = keep.tile([P, P], F32, name="gain_square")
+        nc.gpsimd.memset(gain_square[:], 0.0)
+        moments = keep.tile([P, TILES, 4], F32, name="moments")
+        nc.gpsimd.memset(moments[:], -1.0)
+
+        w_words = {}
+
+        def load_words(part):
+            words = keep.tile([P, 2 * QUARTER], U8, name="w_words%d" % part, align_bytes=64)
+            nc.sync.dma_start(
+                out=words[:].bitcast(I32),
+                in_=w_qkv_words[0][:, 2 * QUARTER * part : 2 * QUARTER * (part + 1)].bitcast(I32),
+            )
+            w_words[part] = words
+
+        def load_scales(plane, c0, c1):
+            for quad in range(4):
+                nc.sync.dma_start(
+                    out=plane[32 * quad : 32 * quad + 4, :].bitcast(I32),
+                    in_=w_qkv_scales[0][4 * quad : 4 * quad + 4, c0:c1].bitcast(I32),
+                )
+
+        load_words(Q_PART)
+        load_scales(first_scales, 0, QUARTER)
+        load_scales(other_scales, QUARTER, COLUMNS)
+        for part in (V1_PART, V2_PART, K_PART):
+            load_words(part)
+
+        nc.scalar.activation(out=gain_square[0:TILES, :], in_=gain_rows[:], func=ACT.Identity)
+
+        x_codes = [keep.tile([P, PIXELS], U32, name="x_codes%d" % b, align_bytes=64) for b in range(MAPS)]
+        x_scales = [keep.tile([P, PIXELS], U8, name="x_scales%d" % b, align_bytes=64) for b in range(MAPS)]
+        grouped = {}
+
+        def turn_input(i):
+            split = keep.tile([P, 2, 2, P], F32, name="split%d" % i, align_bytes=64)
+            nc.vector.tensor_copy(out=split[:], in_=x_rows[i][:].bitcast(F32).rearrange("p j (w u) -> p j u w", u=2))
+            bank = product_banks.tile([P, 2, 2, P], F32, name="bank", tag="product")
+            for j in range(2):
+                for u in range(2):
+                    nc.tensor.transpose(bank[:, j, u, :], split[:, j, u, :], ident[:])
+            grouped[i] = keep.tile([P, 2 * P * 4], BF16, name="grouped%d" % i, align_bytes=64)
+            nc.scalar.copy(
+                out=grouped[i][:].bitcast(F32).rearrange("k (j p u) -> k j p u", j=2, u=2),
+                in_=bank[:].rearrange("k j u p -> k j p u"),
+            )
+
+        def quantize_input(i):
+            b, half = divmod(i, 2)
+            cols = slice(2 * P * half, 2 * P * (half + 1))
+            nc.vector.quantize_mx(out=x_codes[b][:, cols].bitcast(E5M2X4), scales=x_scales[b][:, cols], in_=grouped[i][:])
+
+        turn_input(0)
+        turn_input(1)
+        turn_input(2)
+        quantize_input(0)
+        turn_input(3)
+        quantize_input(1)
+        quantize_input(2)
+        quantize_input(3)
+
+        gain_bank = turned_banks.tile([P, P], F32, name="gain_bank", tag="turned")
+        nc.tensor.transpose(gain_bank[:], gain_square[:], ident[:])
+        minus_gain = keep.tile([P, TILES], F32, name="minus_gain")
+        nc.scalar.activation(out=minus_gain[:], in_=gain_bank[:, 0:TILES], func=ACT.Copy, scale=-1.0)
+
+        products, stats, factors, normed, turned, results = {}, {}, {}, {}, {}, {}
+
+        def multiply(s, b):
+            part, h = order[s]
+            if part == Q_PART:
+                w_scale = first_scales[:, P * h : P * (h + 1)]
+            else:
+                c0 = QUARTER * (part - 1) + P * h
+                w_scale = other_scales[:, c0 : c0 + P]
+            products[s, b] = product_banks.tile([P, PIXELS], F32, name="product", tag="product")
+            nc.tensor.matmul_mx(
+                out=products[s, b][:],
+                lhsT=w_words[part][:, 2 * P * h : 2 * P * (h + 1)].bitcast(E2M1X4),
+                lhsT_scale=w_scale,
+                rhs=x_codes[b][:].bitcast(E5M2X4),
+                rhs_scale=x_scales[b][:],
+                start=True,
+                stop=True,
+            )
+
+        def measure(s, b):
+            if b == 0:
+                stats[s] = small.tile([P, MAPS, 6], F32, name="stats")
+            nc.vector.bn_stats(out=stats[s][:, b, :], in_=products[s, b][:])
+
+        def aggregate(s):
+            nc.vector.bn_aggr(out=moments[:, s, 1:3], in_=stats[s][:].rearrange("p b n -> p (b n)"))
+
+        def make_factors(s):
+            part, h = order[s]
+            c = HEADS * part + h
+            rstd = small.tile([P, 1], F32, name="rstd")
+            nc.scalar.activation(out=rstd[:], in_=moments[:, s, 2:3], func=ACT.Abs_reciprocal_sqrt, bias=BN_EPS)
+            factors[s] = small.tile([P, 2], F32, name="factors")
+            nc.gpsimd.tensor_scalar(
+                out=factors[s][:], in0=moments[:, s, 0:2], scalar1=rstd[:], scalar2=minus_gain[:, c : c + 1], op0=ALU.mult, op1=ALU.mult
+            )
+
+        def normalise(s, b, on_vector):
+            normed[s, b] = work.tile([P, PIXELS], F32, name="normed")
+            scale, shift = factors[s][:, 0:1], factors[s][:, 1:2]
+            if on_vector:
+                nc.vector.tensor_scalar(out=normed[s, b][:], in0=products[s, b][:], scalar1=scale, scalar2=shift, op0=ALU.mult, op1=ALU.add)
+            else:
+                nc.scalar.activation(out=normed[s, b][:], in_=products[s, b][:], func=ACT.Identity, scale=scale, bias=shift)
+
+        def turn(s, b):
+            turned[s, b] = turned_banks.tile([P, ROWS, P], F32, name="turned", tag="turned")
+            for j in range(ROWS):
+                nc.tensor.transpose(turned[s, b][:, j, :], normed[s, b][:, P * j : P * (j + 1)], ident[:])
+
+        def put_out(s, b):
+            part, h = order[s]
+            copy = nc.vector.tensor_copy if b == 0 else nc.scalar.copy
+            if part in (Q_PART, K_PART):
+                result = work.tile([P, ROWS, DIM], F32, name="qk_result")
+                copy(out=result[:], in_=turned[s, b][:])
+                dest = out_0 if part == Q_PART else out_1
+            else:
+                if part == V1_PART:
+                    results[b] = work.tile([P, ROWS, 2 * DIM], F32, name="v_result")
+                result = results[b]
+                half = part - V1_PART
+                copy(out=result[:, :, DIM * half : DIM * (half + 1)], in_=turned[s, b][:])
+                dest = out_2
+            if part != V1_PART:
+                nc.sync.dma_start(out=dest[b, h].rearrange("(p j) d -> p j d", j=ROWS), in_=result[:])
+
+        last = TILES - 1
+
+        def when(step, s, *args):
+            if 0 <= s < TILES:
+                step(s, *args)
+
+        for s in range(-1, TILES + 3):
+            when(make_factors, s - 1)
+            if s - 2 != last:
+                when(normalise, s - 2, 1, False)
+            when(measure, s, 0)
+            when(put_out, s - 3, 1)
+            when(turn, s - 2, 0)
+            when(multiply, s + 1, 0)
+            when(multiply, s + 1, 1)
+            when(turn, s - 2, 1)
+            when(measure, s, 1)
+            when(normalise, s - 1, 0, False)
+            when(put_out, s - 2, 0)
+            if s - 1 == last:
+                normalise(last, 1, True)
+            when(aggregate, s)

@@ -37,8 +37,8 @@ def tile_levitattention_pa_kernel(tc, inputs, w_qkv_words, w_qkv_scales, bn_scal
         keep = ctx.enter_context(tc.tile_pool(name="keep", bufs=1))
         small = ctx.enter_context(tc.tile_pool(name="small", bufs=4))
         work = ctx.enter_context(tc.tile_pool(name="work", bufs=4))
-        product_banks = ctx.enter_context(tc.psum_pool(name="product_banks", bufs=6))
-        turned_banks = ctx.enter_context(tc.psum_pool(name="turned_banks", bufs=2))
+        product_banks = ctx.enter_context(tc.psum_pool(name="product_banks", bufs=4))
+        turned_banks = ctx.enter_context(tc.psum_pool(name="turned_banks", bufs=4))
         ctx.enter_context(tc.manual_schedule())
 
         pixels = inputs.rearrange("b h w c -> b (h w) c")
@@ -61,8 +61,7 @@ def tile_levitattention_pa_kernel(tc, inputs, w_qkv_words, w_qkv_scales, bn_scal
         make_identity(nc, ident[:])
         gain_square = keep.tile([P, P], F32, name="gain_square")
         nc.gpsimd.memset(gain_square[:], 0.0)
-        moments = keep.tile([P, TILES, 4], F32, name="moments")
-        nc.gpsimd.memset(moments[:], -1.0)
+        moments = keep.tile([P, TILES, 2], F32, name="moments")
 
         w_words = {}
 
@@ -87,16 +86,21 @@ def tile_levitattention_pa_kernel(tc, inputs, w_qkv_words, w_qkv_scales, bn_scal
         for part in (V1_PART, V2_PART, K_PART):
             load_words(part)
 
-        nc.scalar.activation(out=gain_square[0:TILES, :], in_=gain_rows[:], func=ACT.Identity)
+        nc.scalar.copy(out=gain_square[0:TILES, :], in_=gain_rows[:])
 
         x_codes = [keep.tile([P, PIXELS], U32, name="x_codes%d" % b, align_bytes=64) for b in range(MAPS)]
         x_scales = [keep.tile([P, PIXELS], U8, name="x_scales%d" % b, align_bytes=64) for b in range(MAPS)]
         grouped = {}
 
+        splits = {}
+
+        def split_input(i):
+            splits[i] = keep.tile([P, 2, 2, P], F32, name="split%d" % i, align_bytes=64)
+            nc.vector.tensor_copy(out=splits[i][:], in_=x_rows[i][:].bitcast(F32).rearrange("p j (w u) -> p j u w", u=2))
+
         def turn_input(i):
-            split = keep.tile([P, 2, 2, P], F32, name="split%d" % i, align_bytes=64)
-            nc.vector.tensor_copy(out=split[:], in_=x_rows[i][:].bitcast(F32).rearrange("p j (w u) -> p j u w", u=2))
-            bank = product_banks.tile([P, 2, 2, P], F32, name="bank", tag="product")
+            split = splits[i]
+            bank = turned_banks.tile([P, 2, 2, P], F32, name="bank", tag="turned")
             for j in range(2):
                 for u in range(2):
                     nc.tensor.transpose(bank[:, j, u, :], split[:, j, u, :], ident[:])
@@ -111,21 +115,14 @@ def tile_levitattention_pa_kernel(tc, inputs, w_qkv_words, w_qkv_scales, bn_scal
             cols = slice(2 * P * half, 2 * P * (half + 1))
             nc.vector.quantize_mx(out=x_codes[b][:, cols].bitcast(E5M2X4), scales=x_scales[b][:, cols], in_=grouped[i][:])
 
-        turn_input(0)
-        turn_input(1)
-        turn_input(2)
-        quantize_input(0)
-        turn_input(3)
-        quantize_input(1)
-        quantize_input(2)
-        quantize_input(3)
-
-        gain_bank = turned_banks.tile([P, P], F32, name="gain_bank", tag="turned")
-        nc.tensor.transpose(gain_bank[:], gain_square[:], ident[:])
         minus_gain = keep.tile([P, TILES], F32, name="minus_gain")
-        nc.scalar.activation(out=minus_gain[:], in_=gain_bank[:, 0:TILES], func=ACT.Copy, scale=-1.0)
 
-        products, stats, factors, normed, turned, results = {}, {}, {}, {}, {}, {}
+        def turn_gain():
+            gain_bank = turned_banks.tile([P, P], F32, name="gain_bank", tag="turned")
+            nc.tensor.transpose(gain_bank[:], gain_square[:], ident[:])
+            nc.vector.tensor_scalar(out=minus_gain[:], in0=gain_bank[:, 0:TILES], scalar1=-1.0, scalar2=None, op0=ALU.mult)
+
+        products, stats, negated, factors, normed, turned, results = {}, {}, {}, {}, {}, {}, {}
 
         def multiply(s, b):
             part, h = order[s]
@@ -150,42 +147,60 @@ def tile_levitattention_pa_kernel(tc, inputs, w_qkv_words, w_qkv_scales, bn_scal
                 stats[s] = small.tile([P, MAPS, 6], F32, name="stats")
             nc.vector.bn_stats(out=stats[s][:, b, :], in_=products[s, b][:])
 
+        def evacuate(s, b):
+            if b == 0:
+                negated[s] = work.tile([P, MAPS, PIXELS], F32, name="negated", bufs=6)
+            nc.scalar.activation(out=negated[s][:, b, :], in_=products[s, b][:], func=ACT.Copy, scale=-1.0)
+
         def aggregate(s):
-            nc.vector.bn_aggr(out=moments[:, s, 1:3], in_=stats[s][:].rearrange("p b n -> p (b n)"))
+            nc.vector.bn_aggr(out=moments[:, s, :], in_=stats[s][:].rearrange("p b n -> p (b n)"))
+
+        def column_tile(s):
+            part, h = order[s]
+            return HEADS * part + h
 
         def make_factors(s):
-            part, h = order[s]
-            c = HEADS * part + h
-            rstd = small.tile([P, 1], F32, name="rstd")
-            nc.scalar.activation(out=rstd[:], in_=moments[:, s, 2:3], func=ACT.Abs_reciprocal_sqrt, bias=BN_EPS)
-            factors[s] = small.tile([P, 2], F32, name="factors")
-            nc.gpsimd.tensor_scalar(
-                out=factors[s][:], in0=moments[:, s, 0:2], scalar1=rstd[:], scalar2=minus_gain[:, c : c + 1], op0=ALU.mult, op1=ALU.mult
-            )
+            if s % 2 == 0:
+                return
+            rstd = small.tile([P, 2], F32, name="rstd")
+            nc.scalar.activation(out=rstd[:], in_=moments[:, s - 1 : s + 1, 1], func=ACT.Abs_reciprocal_sqrt, bias=BN_EPS)
+            c0, c1 = column_tile(s - 1), column_tile(s)
+            pair = small.tile([P, 2], F32, name="pair")
+            nc.gpsimd.tensor_tensor(out=pair[:], in0=rstd[:], in1=minus_gain[:, c0 : c1 + 1 : c1 - c0], op=ALU.mult)
+            factors[s - 1], factors[s] = pair[:, 0:1], pair[:, 1:2]
 
-        def normalise(s, b, on_vector):
-            normed[s, b] = work.tile([P, PIXELS], F32, name="normed")
-            scale, shift = factors[s][:, 0:1], factors[s][:, 1:2]
-            if on_vector:
-                nc.vector.tensor_scalar(out=normed[s, b][:], in0=products[s, b][:], scalar1=scale, scalar2=shift, op0=ALU.mult, op1=ALU.add)
+        def normalise(s):
+            normed[s] = work.tile([P, MAPS, PIXELS], F32, name="normed")
+            if s < TILES - 2:
+                nc.gpsimd.tensor_scalar(
+                    out=normed[s][:], in0=negated[s][:], scalar1=moments[:, s, 0:1], scalar2=factors[s], op0=ALU.add, op1=ALU.mult
+                )
             else:
-                nc.scalar.activation(out=normed[s, b][:], in_=products[s, b][:], func=ACT.Identity, scale=scale, bias=shift)
+                for b in range(MAPS):
+                    nc.vector.tensor_scalar(
+                        out=normed[s][:, b, :],
+                        in0=negated[s][:, b, :],
+                        scalar1=moments[:, s, 0:1],
+                        scalar2=factors[s],
+                        op0=ALU.add,
+                        op1=ALU.mult,
+                    )
 
         def turn(s, b):
             turned[s, b] = turned_banks.tile([P, ROWS, P], F32, name="turned", tag="turned")
             for j in range(ROWS):
-                nc.tensor.transpose(turned[s, b][:, j, :], normed[s, b][:, P * j : P * (j + 1)], ident[:])
+                nc.tensor.transpose(turned[s, b][:, j, :], normed[s][:, b, P * j : P * (j + 1)], ident[:])
 
-        def put_out(s, b):
+        def put_out(s, b, on_vector):
             part, h = order[s]
-            copy = nc.vector.tensor_copy if b == 0 else nc.scalar.copy
+            copy = nc.vector.tensor_copy if on_vector else nc.scalar.copy
             if part in (Q_PART, K_PART):
-                result = work.tile([P, ROWS, DIM], F32, name="qk_result")
+                result = work.tile([P, ROWS, DIM], F32, name="qk_result", bufs=8)
                 copy(out=result[:], in_=turned[s, b][:])
                 dest = out_0 if part == Q_PART else out_1
             else:
                 if part == V1_PART:
-                    results[b] = work.tile([P, ROWS, 2 * DIM], F32, name="v_result")
+                    results[b] = work.tile([P, ROWS, 2 * DIM], F32, name="v_result", bufs=6)
                 result = results[b]
                 half = part - V1_PART
                 copy(out=result[:, :, DIM * half : DIM * (half + 1)], in_=turned[s, b][:])
@@ -193,25 +208,52 @@ def tile_levitattention_pa_kernel(tc, inputs, w_qkv_words, w_qkv_scales, bn_scal
             if part != V1_PART:
                 nc.sync.dma_start(out=dest[b, h].rearrange("(p j) d -> p j d", j=ROWS), in_=result[:])
 
-        last = TILES - 1
-
         def when(step, s, *args):
             if 0 <= s < TILES:
                 step(s, *args)
 
-        for s in range(-1, TILES + 3):
+        for i in range(2 * MAPS):
+            split_input(i)
+            turn_input(i)
+        quantize_input(0)
+        quantize_input(1)
+        multiply(0, 0)
+        multiply(1, 0)
+        quantize_input(2)
+        measure(0, 0)
+        quantize_input(3)
+        multiply(0, 1)
+        evacuate(0, 0)
+        turn_gain()
+
+        last = TILES - 1
+        for s in range(TILES):
+            when(evacuate, s - 1, 1)
             when(make_factors, s - 1)
-            if s - 2 != last:
-                when(normalise, s - 2, 1, False)
-            when(measure, s, 0)
-            when(put_out, s - 3, 1)
-            when(turn, s - 2, 0)
-            when(multiply, s + 1, 0)
+            when(normalise, s - 2)
+            when(measure, s + 1, 0)
+            when(multiply, s + 2, 0)
             when(multiply, s + 1, 1)
-            when(turn, s - 2, 1)
+            when(put_out, s - 4, 0, False)
+            when(turn, s - 3, 0)
+            when(turn, s - 3, 1)
             when(measure, s, 1)
-            when(normalise, s - 1, 0, False)
-            when(put_out, s - 2, 0)
-            if s - 1 == last:
-                normalise(last, 1, True)
+            when(evacuate, s + 1, 0)
+            when(put_out, s - 4, 1, True)
             when(aggregate, s)
+        evacuate(last, 1)
+        make_factors(last)
+        put_out(last - 3, 0, False)
+        put_out(last - 3, 1, True)
+        turn(last - 2, 0)
+        turn(last - 2, 1)
+        normalise(last - 1)
+        normalise(last)
+        put_out(last - 2, 0, False)
+        put_out(last - 2, 1, False)
+        for s in (last - 1, last):
+            turn(s, 0)
+            turn(s, 1)
+        for s in (last - 1, last):
+            put_out(s, 0, False)
+            put_out(s, 1, True)

@@ -4,9 +4,10 @@ import concourse.mybir as mybir
 from concourse.masks import make_identity
 
 MAPS, PIXELS, K, HEADS, DIM = 2, 512, 512, 8, 128
+SAMPLES = MAPS * PIXELS
 COLUMNS = 4 * HEADS * DIM
 BN_EPS = 1e-5
-FLOPS = 2 * MAPS * PIXELS * K * COLUMNS
+FLOPS = 2 * SAMPLES * K * COLUMNS
 
 F32 = mybir.dt.float32
 BF16 = mybir.dt.bfloat16
@@ -20,9 +21,18 @@ ACT = mybir.ActivationFunctionType
 
 P = 128
 ROWS = PIXELS // P
-QUARTER = HEADS * DIM
+PIECES = 2 * MAPS
+PART_COLUMNS = HEADS * DIM
 TILES = COLUMNS // P
 Q_PART, K_PART, V1_PART, V2_PART = range(4)
+
+SQUARES_LAG = 1
+NORMALISE_LAG = 3
+TURN_LAG = 4
+VECTOR_EVACUATES_BOTH = range(2, 7)
+
+SCALED_BUFS, NORMED_BUFS, QK_RESULT_BUFS, V_RESULT_BUFS, FACTOR_BUFS = 7, 4, 8, 6, 4
+PRODUCT_BANKS, TURNED_BANKS = 4, 4
 
 
 def tile_levitattention_pa_kernel(tc, inputs, w_qkv_words, w_qkv_scales, bn_scale, out_0, out_1, out_2):
@@ -35,79 +45,89 @@ def tile_levitattention_pa_kernel(tc, inputs, w_qkv_words, w_qkv_scales, bn_scal
 
     with ExitStack() as ctx:
         keep = ctx.enter_context(tc.tile_pool(name="keep", bufs=1))
-        small = ctx.enter_context(tc.tile_pool(name="small", bufs=4))
-        work = ctx.enter_context(tc.tile_pool(name="work", bufs=4))
-        product_banks = ctx.enter_context(tc.psum_pool(name="product_banks", bufs=4))
-        turned_banks = ctx.enter_context(tc.psum_pool(name="turned_banks", bufs=4))
+        work = ctx.enter_context(tc.tile_pool(name="work", bufs=1))
+        product_banks = ctx.enter_context(tc.psum_pool(name="product_banks", bufs=PRODUCT_BANKS))
+        turned_banks = ctx.enter_context(tc.psum_pool(name="turned_banks", bufs=TURNED_BANKS))
         ctx.enter_context(tc.manual_schedule())
 
         pixels = inputs.rearrange("b h w c -> b (h w) c")
-        x_rows = []
-        for i in range(2 * MAPS):
+        x_rows, w_words = {}, {}
+
+        def load_input(i):
             b, half = divmod(i, 2)
-            rows = keep.tile([P, 2, K], BF16, name="x_rows%d" % i, align_bytes=64)
-            nc.sync.dma_start(out=rows[:], in_=pixels[b].rearrange("(p j) c -> p j c", j=ROWS)[:, 2 * half : 2 * half + 2, :])
-            x_rows.append(rows)
+            x_rows[i] = keep.tile([P, 2, K], BF16, name="x_rows%d" % i, align_bytes=64)
+            by_partition = pixels[b].rearrange("(p j) c -> p j c", j=ROWS)
+            nc.sync.dma_start(out=x_rows[i][:], in_=by_partition[:, 2 * half : 2 * half + 2, :])
+
+        def load_words(part):
+            w_words[part] = keep.tile([P, 2 * PART_COLUMNS], U8, name="w_words%d" % part, align_bytes=64)
+            source = w_qkv_words[0][:, 2 * PART_COLUMNS * part : 2 * PART_COLUMNS * (part + 1)]
+            nc.sync.dma_start(out=w_words[part][:].bitcast(I32), in_=source.bitcast(I32))
+
+        def load_scales(queue, plane, c0, c1):
+            for quad in range(4):
+                source = w_qkv_scales[0][4 * quad : 4 * quad + 4, c0:c1]
+                queue.dma_start(out=plane[32 * quad : 32 * quad + 4, :].bitcast(I32), in_=source.bitcast(I32))
+
+        q_scales = keep.tile([P, PART_COLUMNS], U8, name="q_scales", align_bytes=64)
+        other_scales = keep.tile([P, COLUMNS - PART_COLUMNS], U8, name="other_scales", align_bytes=64)
+        nc.vector.memset(q_scales[:].bitcast(I32), 0)
+        nc.vector.memset(other_scales[:].bitcast(I32), 0)
 
         gain_rows = keep.tile([TILES, P], BF16, name="gain_rows")
+        for i in range(PIECES - 1):
+            load_input(i)
         nc.scalar.dma_start(out=gain_rows[:], in_=bn_scale.rearrange("(c p) -> c p", p=P))
-
-        first_scales = keep.tile([P, QUARTER], U8, name="first_scales", align_bytes=64)
-        other_scales = keep.tile([P, COLUMNS - QUARTER], U8, name="other_scales", align_bytes=64)
-        nc.vector.memset(first_scales[:].bitcast(I32), 0)
-        nc.vector.memset(other_scales[:].bitcast(I32), 0)
+        load_scales(nc.scalar, q_scales, 0, PART_COLUMNS)
+        load_input(PIECES - 1)
+        load_words(Q_PART)
+        load_scales(nc.sync, other_scales, PART_COLUMNS, COLUMNS)
+        for part in (V1_PART, V2_PART, K_PART):
+            load_words(part)
 
         ident = keep.tile([P, P], F32, name="ident")
         make_identity(nc, ident[:])
         gain_square = keep.tile([P, P], F32, name="gain_square")
         nc.gpsimd.memset(gain_square[:], 0.0)
         moments = keep.tile([P, TILES, 2], F32, name="moments")
+        multipliers = keep.tile([P, TILES, 2], F32, name="multipliers")
+        nc.gpsimd.memset(multipliers[:], -1.0 / SAMPLES)
+        first_sums = keep.tile([P, TILES], F32, name="first_sums")
+        square_sums = keep.tile([P, TILES], F32, name="square_sums")
+        squares = keep.tile([P, MAPS, PIXELS], F32, name="squares")
 
-        w_words = {}
+        table_warm_up = keep.tile([P, 1], F32, name="table_warm_up")
+        nc.scalar.activation(out=table_warm_up[:], in_=multipliers[:, 0, 0:1], func=ACT.Abs_reciprocal_sqrt)
 
-        def load_words(part):
-            words = keep.tile([P, 2 * QUARTER], U8, name="w_words%d" % part, align_bytes=64)
-            nc.sync.dma_start(
-                out=words[:].bitcast(I32),
-                in_=w_qkv_words[0][:, 2 * QUARTER * part : 2 * QUARTER * (part + 1)].bitcast(I32),
-            )
-            w_words[part] = words
+        nc.scalar.activation(out=gain_square[0:TILES, :], in_=gain_rows[:], func=ACT.Copy)
 
-        def load_scales(plane, c0, c1):
-            for quad in range(4):
-                nc.sync.dma_start(
-                    out=plane[32 * quad : 32 * quad + 4, :].bitcast(I32),
-                    in_=w_qkv_scales[0][4 * quad : 4 * quad + 4, c0:c1].bitcast(I32),
-                )
-
-        load_words(Q_PART)
-        load_scales(first_scales, 0, QUARTER)
-        load_scales(other_scales, QUARTER, COLUMNS)
-        for part in (V1_PART, V2_PART, K_PART):
-            load_words(part)
-
-        nc.scalar.copy(out=gain_square[0:TILES, :], in_=gain_rows[:])
+        def turn_gain():
+            gain_bank = turned_banks.tile([P, P], F32, name="gain_bank", tag="turned")
+            nc.tensor.transpose(gain_bank[:], gain_square[:], ident[:])
+            v_steps = multipliers[:, HEADS : 3 * HEADS, 1].rearrange("p (h half) -> p h half", half=2)
+            v_tiles = gain_bank[:, 2 * HEADS : 4 * HEADS].rearrange("p (half h) -> p h half", half=2)
+            for steps, tiles in (
+                (multipliers[:, 0:HEADS, 1], gain_bank[:, 0:HEADS]),
+                (v_steps, v_tiles),
+                (multipliers[:, 3 * HEADS : 4 * HEADS, 1], gain_bank[:, HEADS : 2 * HEADS]),
+            ):
+                nc.vector.tensor_scalar(out=steps, in0=tiles, scalar1=float(SAMPLES), scalar2=None, op0=ALU.mult)
 
         x_codes = [keep.tile([P, PIXELS], U32, name="x_codes%d" % b, align_bytes=64) for b in range(MAPS)]
         x_scales = [keep.tile([P, PIXELS], U8, name="x_scales%d" % b, align_bytes=64) for b in range(MAPS)]
         grouped = {}
 
-        splits = {}
-
-        def split_input(i):
-            splits[i] = keep.tile([P, 2, 2, P], F32, name="split%d" % i, align_bytes=64)
-            nc.vector.tensor_copy(out=splits[i][:], in_=x_rows[i][:].bitcast(F32).rearrange("p j (w u) -> p j u w", u=2))
-
         def turn_input(i):
-            split = splits[i]
+            split = keep.tile([P, 2, 2, P], F32, name="split%d" % i, align_bytes=64)
+            nc.vector.tensor_copy(out=split[:], in_=x_rows[i][:].bitcast(F32).rearrange("p j (w u) -> p j u w", u=2))
             bank = turned_banks.tile([P, 2, 2, P], F32, name="bank", tag="turned")
             for j in range(2):
                 for u in range(2):
                     nc.tensor.transpose(bank[:, j, u, :], split[:, j, u, :], ident[:])
             grouped[i] = keep.tile([P, 2 * P * 4], BF16, name="grouped%d" % i, align_bytes=64)
             nc.scalar.copy(
-                out=grouped[i][:].bitcast(F32).rearrange("k (j p u) -> k j p u", j=2, u=2),
-                in_=bank[:].rearrange("k j u p -> k j p u"),
+                out=grouped[i][:].bitcast(F32).rearrange("w (j p u) -> w j p u", j=2, u=2),
+                in_=bank[:].rearrange("w j u p -> w j p u"),
             )
 
         def quantize_input(i):
@@ -115,21 +135,14 @@ def tile_levitattention_pa_kernel(tc, inputs, w_qkv_words, w_qkv_scales, bn_scal
             cols = slice(2 * P * half, 2 * P * (half + 1))
             nc.vector.quantize_mx(out=x_codes[b][:, cols].bitcast(E5M2X4), scales=x_scales[b][:, cols], in_=grouped[i][:])
 
-        minus_gain = keep.tile([P, TILES], F32, name="minus_gain")
-
-        def turn_gain():
-            gain_bank = turned_banks.tile([P, P], F32, name="gain_bank", tag="turned")
-            nc.tensor.transpose(gain_bank[:], gain_square[:], ident[:])
-            nc.vector.tensor_scalar(out=minus_gain[:], in0=gain_bank[:, 0:TILES], scalar1=-1.0, scalar2=None, op0=ALU.mult)
-
-        products, stats, negated, factors, normed, turned, results = {}, {}, {}, {}, {}, {}, {}
+        products, scaled, factors, normed, turned, v_results = {}, {}, {}, {}, {}, {}
 
         def multiply(s, b):
             part, h = order[s]
             if part == Q_PART:
-                w_scale = first_scales[:, P * h : P * (h + 1)]
+                w_scale = q_scales[:, P * h : P * (h + 1)]
             else:
-                c0 = QUARTER * (part - 1) + P * h
+                c0 = PART_COLUMNS * (part - 1) + P * h
                 w_scale = other_scales[:, c0 : c0 + P]
             products[s, b] = product_banks.tile([P, PIXELS], F32, name="product", tag="product")
             nc.tensor.matmul_mx(
@@ -142,52 +155,61 @@ def tile_levitattention_pa_kernel(tc, inputs, w_qkv_words, w_qkv_scales, bn_scal
                 stop=True,
             )
 
-        def measure(s, b):
-            if b == 0:
-                stats[s] = small.tile([P, MAPS, 6], F32, name="stats")
-            nc.vector.bn_stats(out=stats[s][:, b, :], in_=products[s, b][:])
-
         def evacuate(s, b):
             if b == 0:
-                negated[s] = work.tile([P, MAPS, PIXELS], F32, name="negated", bufs=6)
-            nc.scalar.activation(out=negated[s][:, b, :], in_=products[s, b][:], func=ACT.Copy, scale=-1.0)
-
-        def aggregate(s):
-            nc.vector.bn_aggr(out=moments[:, s, :], in_=stats[s][:].rearrange("p b n -> p (b n)"))
-
-        def column_tile(s):
-            part, h = order[s]
-            return HEADS * part + h
-
-        def make_factors(s):
-            if s % 2 == 0:
-                return
-            rstd = small.tile([P, 2], F32, name="rstd")
-            nc.scalar.activation(out=rstd[:], in_=moments[:, s - 1 : s + 1, 1], func=ACT.Abs_reciprocal_sqrt, bias=BN_EPS)
-            c0, c1 = column_tile(s - 1), column_tile(s)
-            pair = small.tile([P, 2], F32, name="pair")
-            nc.gpsimd.tensor_tensor(out=pair[:], in0=rstd[:], in1=minus_gain[:, c0 : c1 + 1 : c1 - c0], op=ALU.mult)
-            factors[s - 1], factors[s] = pair[:, 0:1], pair[:, 1:2]
-
-        def normalise(s):
-            normed[s] = work.tile([P, MAPS, PIXELS], F32, name="normed")
-            if s < TILES - 2:
-                nc.gpsimd.tensor_scalar(
-                    out=normed[s][:], in0=negated[s][:], scalar1=moments[:, s, 0:1], scalar2=factors[s], op0=ALU.add, op1=ALU.mult
+                scaled[s] = work.tile([P, MAPS, PIXELS], F32, name="scaled", bufs=SCALED_BUFS)
+            first_sum = first_sums[:, s : s + 1]
+            if b == 0 and s not in VECTOR_EVACUATES_BOTH:
+                nc.scalar.activation(
+                    out=scaled[s][:, 0, :], in_=products[s, 0][:], func=ACT.Copy, scale=1.0 / SAMPLES, accum_out=first_sum
                 )
             else:
+                nc.vector.tensor_scalar(
+                    out=scaled[s][:, b, :],
+                    in0=products[s, b][:],
+                    scalar1=1.0 / SAMPLES,
+                    scalar2=first_sum if b == 1 else None,
+                    op0=ALU.mult,
+                    op1=ALU.add,
+                    accum_out=moments[:, s, 0:1] if b == 1 else first_sum,
+                )
+
+        def sum_squares(s):
+            nc.scalar.activation(
+                out=squares[:],
+                in_=scaled[s][:],
+                func=ACT.Square,
+                scale=-float(SAMPLES),
+                bias=moments[:, s, 0:1],
+                accum_out=square_sums[:, s : s + 1],
+            )
+
+        def make_factors(s0, s1):
+            nc.scalar.activation(
+                out=moments[:, s0:s1, 1],
+                in_=square_sums[:, s0:s1],
+                func=ACT.Abs_reciprocal_sqrt,
+                scale=1.0 / SAMPLES,
+                bias=BN_EPS,
+            )
+            pairs = work.tile([P, s1 - s0, 2], F32, name="pairs", bufs=FACTOR_BUFS)
+            nc.gpsimd.tensor_tensor(out=pairs[:], in0=moments[:, s0:s1, :], in1=multipliers[:, s0:s1, :], op=ALU.mult)
+            for s in range(s0, s1):
+                factors[s] = pairs[:, s - s0, :]
+
+        def normalise(s, on_vector):
+            normed[s] = work.tile([P, MAPS, PIXELS], F32, name="normed", bufs=NORMED_BUFS)
+            shift, scale = factors[s][:, 0:1], factors[s][:, 1:2]
+            if on_vector:
                 for b in range(MAPS):
                     nc.vector.tensor_scalar(
-                        out=normed[s][:, b, :],
-                        in0=negated[s][:, b, :],
-                        scalar1=moments[:, s, 0:1],
-                        scalar2=factors[s],
-                        op0=ALU.add,
-                        op1=ALU.mult,
+                        out=normed[s][:, b, :], in0=scaled[s][:, b, :], scalar1=shift, scalar2=scale, op0=ALU.add, op1=ALU.mult
                     )
+            else:
+                nc.gpsimd.tensor_scalar(out=normed[s][:], in0=scaled[s][:], scalar1=shift, scalar2=scale, op0=ALU.add, op1=ALU.mult)
 
-        def turn(s, b):
-            turned[s, b] = turned_banks.tile([P, ROWS, P], F32, name="turned", tag="turned")
+        def turn(s, b, banks, tag):
+            turned[s, b] = banks.tile([P, ROWS, P], F32, name="turned", tag=tag)
             for j in range(ROWS):
                 nc.tensor.transpose(turned[s, b][:, j, :], normed[s][:, b, P * j : P * (j + 1)], ident[:])
 
@@ -195,65 +217,65 @@ def tile_levitattention_pa_kernel(tc, inputs, w_qkv_words, w_qkv_scales, bn_scal
             part, h = order[s]
             copy = nc.vector.tensor_copy if on_vector else nc.scalar.copy
             if part in (Q_PART, K_PART):
-                result = work.tile([P, ROWS, DIM], F32, name="qk_result", bufs=8)
+                result = work.tile([P, ROWS, DIM], F32, name="qk_result", bufs=QK_RESULT_BUFS)
                 copy(out=result[:], in_=turned[s, b][:])
                 dest = out_0 if part == Q_PART else out_1
             else:
                 if part == V1_PART:
-                    results[b] = work.tile([P, ROWS, 2 * DIM], F32, name="v_result", bufs=6)
-                result = results[b]
+                    v_results[b] = work.tile([P, ROWS, 2 * DIM], F32, name="v_result", bufs=V_RESULT_BUFS)
+                result = v_results[b]
                 half = part - V1_PART
                 copy(out=result[:, :, DIM * half : DIM * (half + 1)], in_=turned[s, b][:])
                 dest = out_2
             if part != V1_PART:
                 nc.sync.dma_start(out=dest[b, h].rearrange("(p j) d -> p j d", j=ROWS), in_=result[:])
 
-        def when(step, s, *args):
+        def when(stage, s, *args):
             if 0 <= s < TILES:
-                step(s, *args)
+                stage(s, *args)
 
-        for i in range(2 * MAPS):
-            split_input(i)
+        for i in range(PIECES):
             turn_input(i)
         quantize_input(0)
         quantize_input(1)
         multiply(0, 0)
         multiply(1, 0)
         quantize_input(2)
-        measure(0, 0)
+        evacuate(0, 0)
         quantize_input(3)
         multiply(0, 1)
-        evacuate(0, 0)
         turn_gain()
 
-        last = TILES - 1
         for s in range(TILES):
-            when(evacuate, s - 1, 1)
-            when(make_factors, s - 1)
-            when(normalise, s - 2)
-            when(measure, s + 1, 0)
+            when(evacuate, s + 1, 0)
+            if s > SQUARES_LAG and s % 2 == 0:
+                make_factors(max(s - NORMALISE_LAG, 0), s - SQUARES_LAG)
+            when(normalise, s - NORMALISE_LAG, False)
+            evacuate(s, 1)
             when(multiply, s + 2, 0)
             when(multiply, s + 1, 1)
-            when(put_out, s - 4, 0, False)
-            when(turn, s - 3, 0)
-            when(turn, s - 3, 1)
-            when(measure, s, 1)
-            when(evacuate, s + 1, 0)
-            when(put_out, s - 4, 1, True)
-            when(aggregate, s)
-        evacuate(last, 1)
-        make_factors(last)
-        put_out(last - 3, 0, False)
-        put_out(last - 3, 1, True)
-        turn(last - 2, 0)
-        turn(last - 2, 1)
-        normalise(last - 1)
-        normalise(last)
-        put_out(last - 2, 0, False)
-        put_out(last - 2, 1, False)
-        for s in (last - 1, last):
-            turn(s, 0)
-            turn(s, 1)
-        for s in (last - 1, last):
+            when(turn, s - TURN_LAG, 0, turned_banks, "turned")
+            when(turn, s - TURN_LAG, 1, turned_banks, "turned")
+            when(sum_squares, s - SQUARES_LAG)
+            when(put_out, s - TURN_LAG - 1, 1, True)
+            when(put_out, s - TURN_LAG, 0, True)
+
+        last = TILES - 1
+        make_factors(TILES - NORMALISE_LAG, last)
+        sum_squares(last)
+        make_factors(last, TILES)
+        put_out(last - TURN_LAG, 1, True)
+        for b in range(MAPS):
+            turn(TILES - TURN_LAG, b, turned_banks, "turned")
+        put_out(TILES - TURN_LAG, 0, True)
+        for s in range(TILES - NORMALISE_LAG, TILES):
+            normalise(s, True)
+            for b in range(MAPS):
+                if s < last - 1:
+                    turn(s, b, turned_banks, "turned")
+                else:
+                    turn(s, b, product_banks, "product")
+        put_out(TILES - TURN_LAG, 1, False)
+        for s in range(TILES - NORMALISE_LAG, TILES):
             put_out(s, 0, False)
             put_out(s, 1, True)

from contextlib import ExitStack

import concourse.mybir as mybir
from concourse.masks import make_identity

MAPS, PIXELS, K, HEADS, DIM = 2, 512, 512, 8, 128
SAMPLES = MAPS * PIXELS
COLUMNS = 4 * HEADS * DIM
BN_EPS = 1e-5
FLOPS = 2 * SAMPLES * K * COLUMNS

F32 = mybir.dt.float32
BF16 = mybir.dt.bfloat16
I32 = mybir.dt.int32
U32 = mybir.dt.uint32
U8 = mybir.dt.uint8
E5M2X4 = mybir.dt.float8_e5m2_x4
E2M1X4 = mybir.dt.float4_e2m1fn_x4
ALU = mybir.AluOpType
ACT = mybir.ActivationFunctionType

P = 128
ROWS = PIXELS // P
PIECES = 2 * MAPS
PART_COLUMNS = HEADS * DIM
TILES = COLUMNS // P
Q_PART, K_PART, V1_PART, V2_PART = range(4)

SQUARES_LAG = 1
NORMALISE_LAG = 3
TURN_LAG = 4
VECTOR_EVACUATES_BOTH = range(2, 7)

SCALED_BUFS, NORMED_BUFS, QK_RESULT_BUFS, V_RESULT_BUFS, FACTOR_BUFS = 7, 4, 8, 6, 4
PRODUCT_BANKS, TURNED_BANKS = 4, 4


def tile_levitattention_pa_kernel(tc, inputs, w_qkv_words, w_qkv_scales, bn_scale, out_0, out_1, out_2):
    nc = tc.nc

    order = [(Q_PART, h) for h in range(HEADS)]
    for h in range(HEADS):
        order += [(V1_PART, h), (V2_PART, h)]
    order += [(K_PART, h) for h in range(HEADS)]

    with ExitStack() as ctx:
        keep = ctx.enter_context(tc.tile_pool(name="keep", bufs=1))
        work = ctx.enter_context(tc.tile_pool(name="work", bufs=1))
        product_banks = ctx.enter_context(tc.psum_pool(name="product_banks", bufs=PRODUCT_BANKS))
        turned_banks = ctx.enter_context(tc.psum_pool(name="turned_banks", bufs=TURNED_BANKS))
        ctx.enter_context(tc.manual_schedule())

        pixels = inputs.rearrange("b h w c -> b (h w) c")
        x_rows, w_words = {}, {}

        def load_input(i):
            b, half = divmod(i, 2)
            x_rows[i] = keep.tile([P, 2, K], BF16, name="x_rows%d" % i, align_bytes=64)
            by_partition = pixels[b].rearrange("(p j) c -> p j c", j=ROWS)
            nc.sync.dma_start(out=x_rows[i][:], in_=by_partition[:, 2 * half : 2 * half + 2, :])

        def load_words(part):
            w_words[part] = keep.tile([P, 2 * PART_COLUMNS], U8, name="w_words%d" % part, align_bytes=64)
            source = w_qkv_words[0][:, 2 * PART_COLUMNS * part : 2 * PART_COLUMNS * (part + 1)]
            nc.sync.dma_start(out=w_words[part][:].bitcast(I32), in_=source.bitcast(I32))

        def load_scales(queue, plane, c0, c1):
            for quad in range(4):
                source = w_qkv_scales[0][4 * quad : 4 * quad + 4, c0:c1]
                queue.dma_start(out=plane[32 * quad : 32 * quad + 4, :].bitcast(I32), in_=source.bitcast(I32))

        q_scales = keep.tile([P, PART_COLUMNS], U8, name="q_scales", align_bytes=64)
        other_scales = keep.tile([P, COLUMNS - PART_COLUMNS], U8, name="other_scales", align_bytes=64)
        nc.vector.memset(q_scales[:].bitcast(I32), 0)
        nc.vector.memset(other_scales[:].bitcast(I32), 0)

        gain_rows = keep.tile([TILES, P], BF16, name="gain_rows")
        for i in range(PIECES - 1):
            load_input(i)
        nc.scalar.dma_start(out=gain_rows[:], in_=bn_scale.rearrange("(c p) -> c p", p=P))
        load_scales(nc.scalar, q_scales, 0, PART_COLUMNS)
        load_input(PIECES - 1)
        load_words(Q_PART)
        load_scales(nc.sync, other_scales, PART_COLUMNS, COLUMNS)
        for part in (V1_PART, V2_PART, K_PART):
            load_words(part)

        ident = keep.tile([P, P], F32, name="ident")
        make_identity(nc, ident[:])
        gain_square = keep.tile([P, P], F32, name="gain_square")
        nc.gpsimd.memset(gain_square[:], 0.0)
        moments = keep.tile([P, TILES, 2], F32, name="moments")
        multipliers = keep.tile([P, TILES, 2], F32, name="multipliers")
        nc.gpsimd.memset(multipliers[:], -1.0 / SAMPLES)
        first_sums = keep.tile([P, TILES], F32, name="first_sums")
        square_sums = keep.tile([P, TILES], F32, name="square_sums")
        squares = keep.tile([P, MAPS, PIXELS], F32, name="squares")

        table_warm_up = keep.tile([P, 1], F32, name="table_warm_up")
        nc.scalar.activation(out=table_warm_up[:], in_=multipliers[:, 0, 0:1], func=ACT.Abs_reciprocal_sqrt)

        nc.scalar.activation(out=gain_square[0:TILES, :], in_=gain_rows[:], func=ACT.Copy)

        def turn_gain():
            gain_bank = turned_banks.tile([P, P], F32, name="gain_bank", tag="turned")
            nc.tensor.transpose(gain_bank[:], gain_square[:], ident[:])
            v_steps = multipliers[:, HEADS : 3 * HEADS, 1].rearrange("p (h half) -> p h half", half=2)
            v_tiles = gain_bank[:, 2 * HEADS : 4 * HEADS].rearrange("p (half h) -> p h half", half=2)
            for steps, tiles in (
                (multipliers[:, 0:HEADS, 1], gain_bank[:, 0:HEADS]),
                (v_steps, v_tiles),
                (multipliers[:, 3 * HEADS : 4 * HEADS, 1], gain_bank[:, HEADS : 2 * HEADS]),
            ):
                nc.vector.tensor_scalar(out=steps, in0=tiles, scalar1=float(SAMPLES), scalar2=None, op0=ALU.mult)

        x_codes = [keep.tile([P, PIXELS], U32, name="x_codes%d" % b, align_bytes=64) for b in range(MAPS)]
        x_scales = [keep.tile([P, PIXELS], U8, name="x_scales%d" % b, align_bytes=64) for b in range(MAPS)]
        grouped = {}

        def turn_input(i):
            split = keep.tile([P, 2, 2, P], F32, name="split%d" % i, align_bytes=64)
            nc.vector.tensor_copy(out=split[:], in_=x_rows[i][:].bitcast(F32).rearrange("p j (w u) -> p j u w", u=2))
            bank = turned_banks.tile([P, 2, 2, P], F32, name="bank", tag="turned")
            for j in range(2):
                for u in range(2):
                    nc.tensor.transpose(bank[:, j, u, :], split[:, j, u, :], ident[:])
            grouped[i] = keep.tile([P, 2 * P * 4], BF16, name="grouped%d" % i, align_bytes=64)
            nc.scalar.copy(
                out=grouped[i][:].bitcast(F32).rearrange("w (j p u) -> w j p u", j=2, u=2),
                in_=bank[:].rearrange("w j u p -> w j p u"),
            )

        def quantize_input(i):
            b, half = divmod(i, 2)
            cols = slice(2 * P * half, 2 * P * (half + 1))
            nc.vector.quantize_mx(out=x_codes[b][:, cols].bitcast(E5M2X4), scales=x_scales[b][:, cols], in_=grouped[i][:])

        products, scaled, factors, normed, turned, v_results = {}, {}, {}, {}, {}, {}

        def multiply(s, b):
            part, h = order[s]
            if part == Q_PART:
                w_scale = q_scales[:, P * h : P * (h + 1)]
            else:
                c0 = PART_COLUMNS * (part - 1) + P * h
                w_scale = other_scales[:, c0 : c0 + P]
            products[s, b] = product_banks.tile([P, PIXELS], F32, name="product", tag="product")
            nc.tensor.matmul_mx(
                out=products[s, b][:],
                lhsT=w_words[part][:, 2 * P * h : 2 * P * (h + 1)].bitcast(E2M1X4),
                lhsT_scale=w_scale,
                rhs=x_codes[b][:].bitcast(E5M2X4),
                rhs_scale=x_scales[b][:],
                start=True,
                stop=True,
            )

        def evacuate(s, b):
            if b == 0:
                scaled[s] = work.tile([P, MAPS, PIXELS], F32, name="scaled", bufs=SCALED_BUFS)
            first_sum = first_sums[:, s : s + 1]
            if b == 0 and s not in VECTOR_EVACUATES_BOTH:
                nc.scalar.activation(
                    out=scaled[s][:, 0, :], in_=products[s, 0][:], func=ACT.Copy, scale=1.0 / SAMPLES, accum_out=first_sum
                )
            else:
                nc.vector.tensor_scalar(
                    out=scaled[s][:, b, :],
                    in0=products[s, b][:],
                    scalar1=1.0 / SAMPLES,
                    scalar2=first_sum if b == 1 else None,
                    op0=ALU.mult,
                    op1=ALU.add,
                    accum_out=moments[:, s, 0:1] if b == 1 else first_sum,
                )

        def sum_squares(s):
            nc.scalar.activation(
                out=squares[:],
                in_=scaled[s][:],
                func=ACT.Square,
                scale=-float(SAMPLES),
                bias=moments[:, s, 0:1],
                accum_out=square_sums[:, s : s + 1],
            )

        def make_factors(s0, s1):
            nc.scalar.activation(
                out=moments[:, s0:s1, 1],
                in_=square_sums[:, s0:s1],
                func=ACT.Abs_reciprocal_sqrt,
                scale=1.0 / SAMPLES,
                bias=BN_EPS,
            )
            pairs = work.tile([P, s1 - s0, 2], F32, name="pairs", bufs=FACTOR_BUFS)
            nc.gpsimd.tensor_tensor(out=pairs[:], in0=moments[:, s0:s1, :], in1=multipliers[:, s0:s1, :], op=ALU.mult)
            for s in range(s0, s1):
                factors[s] = pairs[:, s - s0, :]

        def normalise(s, on_vector):
            normed[s] = work.tile([P, MAPS, PIXELS], F32, name="normed", bufs=NORMED_BUFS)
            shift, scale = factors[s][:, 0:1], factors[s][:, 1:2]
            if on_vector:
                for b in range(MAPS):
                    nc.vector.tensor_scalar(
                        out=normed[s][:, b, :], in0=scaled[s][:, b, :], scalar1=shift, scalar2=scale, op0=ALU.add, op1=ALU.mult
                    )
            else:
                nc.gpsimd.tensor_scalar(out=normed[s][:], in0=scaled[s][:], scalar1=shift, scalar2=scale, op0=ALU.add, op1=ALU.mult)

        def turn(s, b, banks, tag):
            turned[s, b] = banks.tile([P, ROWS, P], F32, name="turned", tag=tag)
            for j in range(ROWS):
                nc.tensor.transpose(turned[s, b][:, j, :], normed[s][:, b, P * j : P * (j + 1)], ident[:])

        def put_out(s, b, on_vector):
            part, h = order[s]
            copy = nc.vector.tensor_copy if on_vector else nc.scalar.copy
            if part in (Q_PART, K_PART):
                result = work.tile([P, ROWS, DIM], F32, name="qk_result", bufs=QK_RESULT_BUFS)
                copy(out=result[:], in_=turned[s, b][:])
                dest = out_0 if part == Q_PART else out_1
            else:
                if part == V1_PART:
                    v_results[b] = work.tile([P, ROWS, 2 * DIM], F32, name="v_result", bufs=V_RESULT_BUFS)
                result = v_results[b]
                half = part - V1_PART
                copy(out=result[:, :, DIM * half : DIM * (half + 1)], in_=turned[s, b][:])
                dest = out_2
            if part != V1_PART:
                nc.sync.dma_start(out=dest[b, h].rearrange("(p j) d -> p j d", j=ROWS), in_=result[:])

        def when(stage, s, *args):
            if 0 <= s < TILES:
                stage(s, *args)

        for i in range(PIECES):
            turn_input(i)
        quantize_input(0)
        quantize_input(1)
        multiply(0, 0)
        multiply(1, 0)
        quantize_input(2)
        evacuate(0, 0)
        quantize_input(3)
        multiply(0, 1)
        turn_gain()

        for s in range(TILES):
            when(evacuate, s + 1, 0)
            if s > SQUARES_LAG and s % 2 == 0:
                make_factors(max(s - NORMALISE_LAG, 0), s - SQUARES_LAG)
            when(normalise, s - NORMALISE_LAG, False)
            evacuate(s, 1)
            when(multiply, s + 2, 0)
            when(multiply, s + 1, 1)
            when(turn, s - TURN_LAG, 0, turned_banks, "turned")
            when(turn, s - TURN_LAG, 1, turned_banks, "turned")
            when(sum_squares, s - SQUARES_LAG)
            when(put_out, s - TURN_LAG - 1, 1, True)
            when(put_out, s - TURN_LAG, 0, True)

        last = TILES - 1
        make_factors(TILES - NORMALISE_LAG, last)
        sum_squares(last)
        make_factors(last, TILES)
        put_out(last - TURN_LAG, 1, True)
        for b in range(MAPS):
            turn(TILES - TURN_LAG, b, turned_banks, "turned")
        put_out(TILES - TURN_LAG, 0, True)
        for s in range(TILES - NORMALISE_LAG, TILES):
            normalise(s, True)
            for b in range(MAPS):
                if s < last - 1:
                    turn(s, b, turned_banks, "turned")
                else:
                    turn(s, b, product_banks, "product")
        put_out(TILES - TURN_LAG, 1, False)
        for s in range(TILES - NORMALISE_LAG, TILES):
            put_out(s, 0, False)
            put_out(s, 1, True)
